import numpy as np
import ml_dtypes


def mxq(x, axis, fmt="e4m3"):
    dtype, down = {"e4m3": (ml_dtypes.float8_e4m3fn, 7), "e5m2": (ml_dtypes.float8_e5m2, 14)}[fmt]
    v = np.moveaxis(np.asarray(x, np.float32).astype(ml_dtypes.bfloat16).astype(np.float64), axis, -1)
    blocks = v.reshape(v.shape[:-1] + (-1, 32))
    amax = np.abs(blocks).max(-1, keepdims=True)
    byte = np.maximum(np.where(amax > 0, np.frexp(amax)[1] - 1 + 127, 0) - down, 1)
    scale = np.exp2(byte - 127.0)
    codes = (blocks / scale).astype(np.float32).astype(dtype).astype(np.float64)
    return np.moveaxis((codes * scale).reshape(v.shape), -1, axis)


BF16 = ml_dtypes.bfloat16


def bf(x):
    return np.asarray(x, np.float32).astype(BF16)


def f64(x):
    return np.asarray(x).astype(np.float64)


B, C, H, W, K, G = 2, 512, 8, 16, 16384, 8
N = B * H * W
EPS = 1e-12


def l2norm(v):
    n = np.sqrt((v * v).sum(-1, keepdims=True))
    return v / np.maximum(n, EPS)


def setup_inputs():
    cen = np.random.standard_normal((G, C))
    sgn = np.sign(np.random.standard_normal((K, 1)))
    gain = np.exp(0.5 * np.random.standard_normal((K, 1)))
    memory = 0.5 * gain * (2.0 * sgn * cen[np.random.randint(0, G, K)] + np.random.standard_normal((K, C)))
    amp = 3.0 * np.random.random((N, 1))
    feat = amp * cen[np.random.randint(0, G, N)] + np.random.standard_normal((N, C))
    x = np.ascontiguousarray(feat.reshape(B, H, W, C).transpose(0, 3, 1, 2))
    return {"x": bf(x), "memory": bf(memory)}


def reference(x, memory):
    feat = f64(x).transpose(0, 2, 3, 1).reshape(N, C)
    feat_norm = l2norm(feat)
    mem_norm = l2norm(f64(memory))
    sim = mxq(feat_norm, 1, "e4m3") @ mxq(mem_norm, 1, "e4m3").T
    e = np.exp(sim - sim.max(1, keepdims=True))
    z = e.sum(1, keepdims=True)
    recon = (mxq(e, 1, "e4m3") @ mxq(mem_norm, 0, "e4m3")) / z
    match_map = (e / z).max(1)
    return recon.reshape(B, H, W, C).transpose(0, 3, 1, 2), match_map.reshape(B, H, W)

@@ -1,0 +1,357 @@
+import concourse.mybir as mybir
+from concourse.masks import make_identity
+
+F32 = mybir.dt.float32
+BF16 = mybir.dt.bfloat16
+U32 = mybir.dt.uint32
+U8 = mybir.dt.uint8
+FP8X4 = mybir.dt.float8_e4m3fn_x4
+ACT = mybir.ActivationFunctionType
+ALU = mybir.AluOpType
+AXIS = mybir.AxisListType
+
+P = 128
+PACK = 4
+HALVES = 2
+BATCH = 2
+CHANNELS = 512
+HW = 128
+PIXELS = BATCH * HW
+SLOTS = 16384
+CHUNK = P * PACK
+N_CHUNKS = SLOTS // CHUNK
+C_TILES = CHANNELS // P
+PLANES_PER_TILE = 4
+EPS = 1e-12
+
+FLOPS = 2 * 2 * PIXELS * SLOTS * CHANNELS
+
+
+def tile_memorybank2d_pa_k_kernel(tc, x, memory, out_0, out_1):
+    nc = tc.nc
+    with tc.manual_schedule(), tc.tile_pool(name="keep", bufs=1) as keep:
+        ident = keep.tile([P, P], F32, name="ident")
+        ones = keep.tile([P, P], F32, name="ones")
+        warm = keep.tile([P, 1], F32, name="warm")
+        fn_codes = keep.tile([P, PIXELS], U32, name="fn_codes", align_bytes=64)
+        fn_scales = keep.tile([P, PIXELS], U8, name="fn_scales", align_bytes=64)
+        chunk_max = keep.tile([P, BATCH, N_CHUNKS], F32, name="chunk_max")
+        chunk_z = keep.tile([P, BATCH, N_CHUNKS], F32, name="chunk_z")
+        neg_max = keep.tile([P, BATCH], F32, name="neg_max")
+        mn = [keep.tile([P, PACK, CHANNELS], BF16, name="mn%d" % g) for g in range(N_CHUNKS)]
+        mnT_codes = [
+            keep.tile([P, CHUNK], U32, name="mnT_codes%d" % g, align_bytes=64)
+            for g in range(N_CHUNKS)
+        ]
+        mnT_planes = [
+            keep.tile([P, CHUNK], U8, name="mnT_planes%d" % j, align_bytes=64)
+            for j in range(N_CHUNKS // PLANES_PER_TILE)
+        ]
+
+        def mnT_scales(g):
+            first_row = PACK * (g % PLANES_PER_TILE)
+            return mnT_planes[g // PLANES_PER_TILE][first_row:P, :]
+
+        def sim_pass(bank, g, b):
+            pixels = slice(b * HW, (b + 1) * HW)
+            nc.tensor.matmul_mx(
+                out=bank,
+                lhsT=fn_codes[:, pixels].bitcast(FP8X4),
+                lhsT_scale=fn_scales[:, pixels],
+                rhs=mnT_codes[g][:].bitcast(FP8X4),
+                rhs_scale=mnT_scales(g),
+                start=True,
+                stop=True,
+            )
+
+        x_sb = keep.tile([P, BATCH, PACK, HW], BF16, name="x_sb")
+        nc.sync.dma_start(
+            out=x_sb[:].rearrange("q b (u e) n -> q b u (e n)", u=HALVES),
+            in_=x.rearrange("b (u q e) h w -> q b u (e h w)", u=HALVES, q=P),
+        )
+        for g in range(N_CHUNKS):
+            rows = memory[g * CHUNK : (g + 1) * CHUNK, :]
+            nc.sync.dma_start(out=mn[g][:], in_=rows.rearrange("(p t) c -> p t c", t=PACK))
+
+        make_identity(nc, ident[:])
+        nc.vector.memset(ones[:], 1.0)
+        nc.vector.memset(warm[:], 1.0)
+        nc.scalar.activation(out=warm[:], in_=warm[:], func=ACT.Sqrt)
+
+        with (
+            tc.tile_pool(name="prep", bufs=1) as prep,
+            tc.tile_pool(name="stats", bufs=4) as stats,
+            tc.tile_pool(name="squares", bufs=4) as squares,
+            tc.tile_pool(name="turned", bufs=3) as turned,
+            tc.psum_pool(name="ps_words", bufs=4) as ps_words,
+            tc.psum_pool(name="ps_sim", bufs=4) as ps_sim,
+        ):
+            x_sq = prep.tile([P, BATCH, PACK, HW], F32, name="x_sq")
+            x_part = prep.tile([P, BATCH, HW], F32, name="x_part")
+            x_norm = prep.tile([P, BATCH, HW], F32, name="x_norm")
+            x_inv = prep.tile([P, BATCH, HW], F32, name="x_inv")
+            fn_grouped = prep.tile([P, BATCH, HW, PACK], BF16, name="fn_grouped", align_bytes=64)
+            x_total = ps_words.tile([P, BATCH, HW], F32, name="x_total", tag="words")
+
+            def pixel_square_sums():
+                nc.vector.tensor_tensor(out=x_sq[:], in0=x_sb[:], in1=x_sb[:], op=ALU.mult)
+                nc.vector.tensor_reduce(
+                    out=x_part[:],
+                    in_=x_sq[:].rearrange("q b t n -> q b n t"),
+                    axis=AXIS.X,
+                    op=ALU.add,
+                )
+                nc.tensor.matmul(
+                    out=x_total[:].rearrange("q b n -> q (b n)"),
+                    lhsT=ones[:],
+                    rhs=x_part[:].rearrange("q b n -> q (b n)"),
+                    start=True,
+                    stop=True,
+                )
+
+            def pixel_codes():
+                nc.vector.tensor_scalar_max(out=x_norm[:], in0=x_norm[:], scalar1=EPS)
+                nc.vector.reciprocal(out=x_inv[:], in_=x_norm[:])
+                nc.vector.tensor_tensor(
+                    out=fn_grouped[:],
+                    in0=x_sb[:].rearrange("q b t n -> q b n t"),
+                    in1=x_inv[:].unsqueeze(3).to_broadcast([P, BATCH, HW, PACK]),
+                    op=ALU.mult,
+                )
+                nc.vector.quantize_mx(
+                    out=fn_codes[:].bitcast(FP8X4),
+                    scales=fn_scales[:],
+                    in_=fn_grouped[:].rearrange("q b n t -> q (b n t)"),
+                )
+
+            norms = {}
+            word_banks = {}
+            turned_words = {}
+            sim_banks = {}
+
+            def slot_norms(g):
+                square_sum = stats.tile([P, PACK], F32, name="square_sum")
+                norms[g] = stats.tile([P, PACK], F32, name="norm")
+                for t in range(PACK):
+                    unread = squares.tile([P, CHANNELS], BF16, name="unread")
+                    nc.scalar.activation(
+                        out=unread[:],
+                        in_=mn[g][:, t, :],
+                        func=ACT.Square,
+                        accum_out=square_sum[:, t : t + 1],
+                    )
+                nc.scalar.activation(out=norms[g][:], in_=square_sum[:], func=ACT.Sqrt)
+
+            def scale_slots(g):
+                floored = stats.tile([P, PACK], F32, name="floored")
+                inverse = stats.tile([P, PACK], F32, name="inverse")
+                nc.vector.tensor_scalar_max(out=floored[:], in0=norms[g][:], scalar1=EPS)
+                nc.vector.reciprocal(out=inverse[:], in_=floored[:])
+                for t in range(PACK):
+                    nc.vector.tensor_scalar_mul(
+                        out=mn[g][:, t, :], in0=mn[g][:, t, :], scalar1=inverse[:, t : t + 1]
+                    )
+
+            def turn_slots(g):
+                words = mn[g][:].bitcast(F32)
+                word_banks[g] = []
+                for u in range(HALVES):
+                    bank = ps_words.tile([P, HALVES, 2, P], F32, name="words")
+                    for a in range(HALVES):
+                        for e in range(2):
+                            nc.tensor.transpose(
+                                bank[:, a, e, :], words[:, 2 * u + e, a * P : (a + 1) * P], ident[:]
+                            )
+                    word_banks[g].append(bank)
+
+            def collect_words(g):
+                turned_words[g] = turned.tile(
+                    [P, HALVES, P, 2, HALVES], F32, name="turned_words", align_bytes=64
+                )
+                nc.scalar.copy(
+                    out=turned_words[g][:, 0], in_=word_banks[g][0][:].rearrange("q a e p -> q p e a")
+                )
+                nc.vector.tensor_copy(
+                    out=turned_words[g][:, 1], in_=word_banks[g][1][:].rearrange("q a e p -> q p e a")
+                )
+
+            def quantise_turned(g):
+                nc.vector.quantize_mx(
+                    out=mnT_codes[g][:].bitcast(FP8X4),
+                    scales=mnT_scales(g),
+                    in_=turned_words[g][:].rearrange("q u p e a -> q (u p e a)").bitcast(BF16),
+                )
+
+            def first_sim(g):
+                sim_banks[g] = []
+                for b in range(BATCH):
+                    bank = ps_sim.tile([P, CHUNK], F32, name="sim")
+                    sim_pass(bank[:], g, b)
+                    sim_banks[g].append(bank)
+
+            def row_max(g):
+                for b in range(BATCH):
+                    nc.vector.tensor_reduce(
+                        out=chunk_max[:, b, g : g + 1], in_=sim_banks[g][b][:], axis=AXIS.X, op=ALU.max
+                    )
+
+            pixel_square_sums()
+            for r in range(N_CHUNKS + 4):
+                if r < N_CHUNKS:
+                    slot_norms(r)
+                if r == 0:
+                    nc.scalar.activation(out=x_norm[:], in_=x_total[:], func=ACT.Sqrt)
+                if 0 <= r - 1 < N_CHUNKS:
+                    scale_slots(r - 1)
+                    turn_slots(r - 1)
+                if r == 1:
+                    pixel_codes()
+                if 0 <= r - 2 < N_CHUNKS:
+                    collect_words(r - 2)
+                if 0 <= r - 3 < N_CHUNKS:
+                    quantise_turned(r - 3)
+                    first_sim(r - 3)
+                if 0 <= r - 4 < N_CHUNKS:
+                    row_max(r - 4)
+
+            nc.scalar.activation(out=warm[:], in_=warm[:], func=ACT.Exp)
+            nc.vector.tensor_reduce(out=neg_max[:], in_=chunk_max[:], axis=AXIS.X, op=ALU.max)
+            nc.vector.tensor_scalar_mul(out=neg_max[:], in0=neg_max[:], scalar1=-1.0)
+
+        with (
+            tc.tile_pool(name="pairs", bufs=2, reuse_waits="tile") as pairs,
+            tc.tile_pool(name="last", bufs=1, reuse_waits="tile") as last,
+            tc.psum_pool(name="ps_recon", bufs=1, reuse_waits="tile") as ps_recon,
+            tc.psum_pool(name="ps_e", bufs=2, reuse_waits="tile") as ps_e,
+        ):
+            recon_banks = [
+                ps_recon.tile([P, BATCH, HW], F32, name="recon%d" % k) for k in range(C_TILES)
+            ]
+            sim_banks = {}
+            e_tiles = {}
+            eT_banks = {}
+            eT_words = {}
+            eT_codes = {}
+            eT_scales = {}
+            mn_grouped = {}
+            mn_codes = {}
+            mn_scales = {}
+
+            def second_sim(g):
+                sim_banks[g] = []
+                for b in range(BATCH):
+                    bank = ps_e.tile([P, CHUNK], F32, name="sim")
+                    sim_pass(bank[:], g, b)
+                    sim_banks[g].append(bank)
+
+            def exponentials(g):
+                e_tiles[g] = []
+                for b in range(BATCH):
+                    e_tile = pairs.tile([P, CHUNK], BF16, name="e%d" % b)
+                    nc.scalar.activation(
+                        out=e_tile[:],
+                        in_=sim_banks[g][b][:],
+                        func=ACT.Exp,
+                        bias=neg_max[:, b : b + 1],
+                        scale=1.0,
+                        accum_out=chunk_z[:, b, g : g + 1],
+                    )
+                    e_tiles[g].append(e_tile)
+
+            def turn_e(g):
+                eT_banks[g] = ps_e.tile([P, HALVES, BATCH, HW], F32, name="eT")
+                for b in range(BATCH):
+                    words = e_tiles[g][b][:].bitcast(F32)
+                    for a in range(HALVES):
+                        nc.tensor.transpose(
+                            eT_banks[g][:, a, b, :], words[:, a * P : (a + 1) * P], ident[:]
+                        )
+
+            def collect_e(g):
+                eT_words[g] = pairs.tile(
+                    [P, BATCH, HW, HALVES], F32, name="eT_words", align_bytes=64
+                )
+                nc.scalar.copy(out=eT_words[g][:], in_=eT_banks[g][:].rearrange("j a b n -> j b n a"))
+
+            def quantise_e(g):
+                eT_codes[g] = pairs.tile([P, PIXELS], U32, name="eT_codes", align_bytes=64)
+                eT_scales[g] = pairs.tile([P, PIXELS], U8, name="eT_scales", align_bytes=64)
+                nc.vector.quantize_mx(
+                    out=eT_codes[g][:].bitcast(FP8X4),
+                    scales=eT_scales[g][:],
+                    in_=eT_words[g][:].rearrange("j b n a -> j (b n a)").bitcast(BF16),
+                )
+
+            def group_slots(g):
+                mn_grouped[g] = pairs.tile(
+                    [P, CHANNELS, PACK], BF16, name="mn_grouped", align_bytes=64
+                )
+                nc.vector.tensor_copy(
+                    out=mn_grouped[g][:].rearrange("p (c i) t -> p c t i", i=4),
+                    in_=mn[g][:].rearrange("p t (c i) -> p c t i", i=4),
+                )
+
+            def quantise_slots(g):
+                mn_codes[g] = pairs.tile([P, CHANNELS], U32, name="mn_codes", align_bytes=64)
+                mn_scales[g] = pairs.tile([P, CHANNELS], U8, name="mn_scales", align_bytes=64)
+                nc.vector.quantize_mx(
+                    out=mn_codes[g][:].bitcast(FP8X4),
+                    scales=mn_scales[g][:],
+                    in_=mn_grouped[g][:].rearrange("p c t -> p (c t)"),
+                )
+
+            def add_to_recon(g):
+                for k in range(C_TILES):
+                    channels = slice(k * P, (k + 1) * P)
+                    nc.tensor.matmul_mx(
+                        out=recon_banks[k][:].rearrange("c b n -> c (b n)"),
+                        lhsT=mn_codes[g][:, channels].bitcast(FP8X4),
+                        lhsT_scale=mn_scales[g][:, channels],
+                        rhs=eT_codes[g][:].bitcast(FP8X4),
+                        rhs_scale=eT_scales[g][:],
+                        start=(g == 0),
+                        stop=(g == N_CHUNKS - 1),
+                    )
+
+            for r in range(N_CHUNKS + 3):
+                if r < N_CHUNKS:
+                    second_sim(r)
+                if 0 <= r - 3 < N_CHUNKS:
+                    add_to_recon(r - 3)
+                if 0 <= r - 1 < N_CHUNKS:
+                    turn_e(r - 1)
+                if r < N_CHUNKS:
+                    exponentials(r)
+                if 0 <= r - 1 < N_CHUNKS:
+                    collect_e(r - 1)
+                    group_slots(r - 1)
+                if 0 <= r - 2 < N_CHUNKS:
+                    quantise_e(r - 2)
+                    quantise_slots(r - 2)
+
+            z = last.tile([P, BATCH], F32, name="z")
+            rz = last.tile([P, BATCH], F32, name="rz")
+            rz_rows = last.tile([P, BATCH, HW], F32, name="rz_rows")
+            rz_bank = ps_e.tile([P, BATCH, HW], F32, name="rz_bank", tag="eT")
+            nc.vector.tensor_reduce(out=z[:], in_=chunk_z[:], axis=AXIS.X, op=ALU.add)
+            nc.vector.reciprocal(out=rz[:], in_=z[:])
+            for b in range(BATCH):
+                nc.tensor.matmul(
+                    out=rz_bank[:, b, :],
+                    lhsT=rz[:, b : b + 1].to_broadcast([P, P]),
+                    rhs=ident[:],
+                    start=True,
+                    stop=True,
+                )
+            nc.scalar.copy(out=rz_rows[:], in_=rz_bank[:])
+            nc.sync.dma_start(
+                out=out_1.rearrange("(o b) h w -> o (b h w)", o=1),
+                in_=rz_rows[0:1].rearrange("o b n -> o (b n)"),
+            )
+            out_tiles = out_0.rearrange("b (k c) h w -> k c b (h w)", c=P)
+            for k in range(C_TILES):
+                recon = last.tile([P, BATCH, HW], F32, name="recon_out%d" % k)
+                nc.vector.tensor_tensor(
+                    out=recon[:], in0=recon_banks[k][:], in1=rz_rows[:], op=ALU.mult
+                )
+                nc.sync.dma_start(out=out_tiles[k], in_=recon[:])

@@ -48,6 +48,9 @@ def tile_memorybank2d_pa_k_kernel(tc, x, memory, out_0, out_1):
             for j in range(N_CHUNKS // PLANES_PER_TILE)
         ]
 
+        def is_chunk(g):
+            return 0 <= g < N_CHUNKS
+
         def mnT_scales(g):
             first_row = PACK * (g % PLANES_PER_TILE)
             return mnT_planes[g // PLANES_PER_TILE][first_row:P, :]
@@ -124,32 +127,38 @@ def tile_memorybank2d_pa_k_kernel(tc, x, memory, out_0, out_1):
                     in_=fn_grouped[:].rearrange("q b n t -> q (b n t)"),
                 )
 
+            square_sums = {}
             norms = {}
+            inverses = {}
             word_banks = {}
             turned_words = {}
             sim_banks = {}
 
-            def slot_norms(g):
-                square_sum = stats.tile([P, PACK], F32, name="square_sum")
-                norms[g] = stats.tile([P, PACK], F32, name="norm")
+            def slot_square_sums(g):
+                square_sums[g] = stats.tile([P, PACK], F32, name="square_sum")
                 for t in range(PACK):
                     unread = squares.tile([P, CHANNELS], BF16, name="unread")
                     nc.scalar.activation(
                         out=unread[:],
                         in_=mn[g][:, t, :],
                         func=ACT.Square,
-                        accum_out=square_sum[:, t : t + 1],
+                        accum_out=square_sums[g][:, t : t + 1],
                     )
-                nc.scalar.activation(out=norms[g][:], in_=square_sum[:], func=ACT.Sqrt)
+
+            def slot_norms(g):
+                norm = stats.tile([P, PACK], F32, name="norm")
+                norms[g] = stats.tile([P, PACK], F32, name="floored")
+                nc.scalar.activation(out=norm[:], in_=square_sums[g][:], func=ACT.Sqrt)
+                nc.gpsimd.tensor_scalar_max(out=norms[g][:], in0=norm[:], scalar1=EPS)
+
+            def invert_norms(g):
+                inverses[g] = stats.tile([P, PACK], F32, name="inverse")
+                nc.vector.reciprocal(out=inverses[g][:], in_=norms[g][:])
 
             def scale_slots(g):
-                floored = stats.tile([P, PACK], F32, name="floored")
-                inverse = stats.tile([P, PACK], F32, name="inverse")
-                nc.vector.tensor_scalar_max(out=floored[:], in0=norms[g][:], scalar1=EPS)
-                nc.vector.reciprocal(out=inverse[:], in_=floored[:])
                 for t in range(PACK):
                     nc.vector.tensor_scalar_mul(
-                        out=mn[g][:, t, :], in0=mn[g][:, t, :], scalar1=inverse[:, t : t + 1]
+                        out=mn[g][:, t, :], in0=mn[g][:, t, :], scalar1=inverses[g][:, t : t + 1]
                     )
 
             def turn_slots(g):
@@ -196,23 +205,28 @@ def tile_memorybank2d_pa_k_kernel(tc, x, memory, out_0, out_1):
                     )
 
             pixel_square_sums()
-            for r in range(N_CHUNKS + 4):
-                if r < N_CHUNKS:
+            for r in range(N_CHUNKS + 5):
+                if is_chunk(r - 5):
+                    first_sim(r - 5)
+                if is_chunk(r):
+                    slot_square_sums(r)
+                if is_chunk(r - 2):
+                    scale_slots(r - 2)
+                    turn_slots(r - 2)
+                if is_chunk(r - 3):
+                    collect_words(r - 3)
+                if is_chunk(r):
                     slot_norms(r)
                 if r == 0:
                     nc.scalar.activation(out=x_norm[:], in_=x_total[:], func=ACT.Sqrt)
-                if 0 <= r - 1 < N_CHUNKS:
-                    scale_slots(r - 1)
-                    turn_slots(r - 1)
+                if is_chunk(r - 1):
+                    invert_norms(r - 1)
                 if r == 1:
                     pixel_codes()
-                if 0 <= r - 2 < N_CHUNKS:
-                    collect_words(r - 2)
-                if 0 <= r - 3 < N_CHUNKS:
-                    quantise_turned(r - 3)
-                    first_sim(r - 3)
-                if 0 <= r - 4 < N_CHUNKS:
-                    row_max(r - 4)
+                if is_chunk(r - 4):
+                    quantise_turned(r - 4)
+                if is_chunk(r - 5):
+                    row_max(r - 5)
 
             nc.scalar.activation(out=warm[:], in_=warm[:], func=ACT.Exp)
             nc.vector.tensor_reduce(out=neg_max[:], in_=chunk_max[:], axis=AXIS.X, op=ALU.max)
@@ -313,41 +327,52 @@ def tile_memorybank2d_pa_k_kernel(tc, x, memory, out_0, out_1):
                         stop=(g == N_CHUNKS - 1),
                     )
 
-            for r in range(N_CHUNKS + 3):
-                if r < N_CHUNKS:
-                    second_sim(r)
-                if 0 <= r - 3 < N_CHUNKS:
-                    add_to_recon(r - 3)
-                if 0 <= r - 1 < N_CHUNKS:
-                    turn_e(r - 1)
-                if r < N_CHUNKS:
-                    exponentials(r)
-                if 0 <= r - 1 < N_CHUNKS:
-                    collect_e(r - 1)
-                    group_slots(r - 1)
-                if 0 <= r - 2 < N_CHUNKS:
-                    quantise_e(r - 2)
-                    quantise_slots(r - 2)
+            rz_rows = last.tile([P, BATCH, HW], F32, name="rz_rows")
 
             z = last.tile([P, BATCH], F32, name="z")
             rz = last.tile([P, BATCH], F32, name="rz")
-            rz_rows = last.tile([P, BATCH, HW], F32, name="rz_rows")
-            rz_bank = ps_e.tile([P, BATCH, HW], F32, name="rz_bank", tag="eT")
-            nc.vector.tensor_reduce(out=z[:], in_=chunk_z[:], axis=AXIS.X, op=ALU.add)
-            nc.vector.reciprocal(out=rz[:], in_=z[:])
-            for b in range(BATCH):
-                nc.tensor.matmul(
-                    out=rz_bank[:, b, :],
-                    lhsT=rz[:, b : b + 1].to_broadcast([P, P]),
-                    rhs=ident[:],
-                    start=True,
-                    stop=True,
+
+            def invert_z():
+                nc.vector.tensor_reduce(out=z[:], in_=chunk_z[:], axis=AXIS.X, op=ALU.add)
+                nc.vector.reciprocal(out=rz[:], in_=z[:])
+
+            def spread_inverse_z():
+                rz_bank = ps_e.tile([P, BATCH, HW], F32, name="rz_bank", tag="sim")
+                for b in range(BATCH):
+                    nc.tensor.matmul(
+                        out=rz_bank[:, b, :],
+                        lhsT=rz[:, b : b + 1].to_broadcast([P, P]),
+                        rhs=ident[:],
+                        start=True,
+                        stop=True,
+                    )
+                nc.scalar.copy(out=rz_rows[:], in_=rz_bank[:])
+                nc.sync.dma_start(
+                    out=out_1.rearrange("(o b) h w -> o (b h w)", o=1),
+                    in_=rz_rows[0:1].rearrange("o b n -> o (b n)"),
                 )
-            nc.scalar.copy(out=rz_rows[:], in_=rz_bank[:])
-            nc.sync.dma_start(
-                out=out_1.rearrange("(o b) h w -> o (b h w)", o=1),
-                in_=rz_rows[0:1].rearrange("o b n -> o (b n)"),
-            )
+
+            for r in range(N_CHUNKS + 4):
+                if is_chunk(r):
+                    second_sim(r)
+                if is_chunk(r - 4):
+                    add_to_recon(r - 4)
+                if is_chunk(r - 1):
+                    turn_e(r - 1)
+                if is_chunk(r - 2):
+                    collect_e(r - 2)
+                if is_chunk(r):
+                    exponentials(r)
+                if is_chunk(r - 2):
+                    group_slots(r - 2)
+                if is_chunk(r - 3):
+                    quantise_e(r - 3)
+                    quantise_slots(r - 3)
+                if r == N_CHUNKS:
+                    invert_z()
+                if r == N_CHUNKS + 1:
+                    spread_inverse_z()
+
             out_tiles = out_0.rearrange("b (k c) h w -> k c b (h w)", c=P)
             for k in range(C_TILES):
                 recon = last.tile([P, BATCH, HW], F32, name="recon_out%d" % k)

@@ -23,6 +23,7 @@ N_CHUNKS = SLOTS // CHUNK
 C_TILES = CHANNELS // P
 PLANES_PER_TILE = 4
 EPS = 1e-12
+BOTH_TO_SCALAR_EVERY = 4
 
 FLOPS = 2 * 2 * PIXELS * SLOTS * CHANNELS
 
@@ -67,14 +68,23 @@ def tile_memorybank2d_pa_k_kernel(tc, x, memory, out_0, out_1):
                 stop=True,
             )
 
+        def spread_column(rows, column):
+            nc.tensor.matmul(
+                out=rows, lhsT=column.to_broadcast([P, P]), rhs=ident[:], start=True, stop=True
+            )
+
         x_sb = keep.tile([P, BATCH, PACK, HW], BF16, name="x_sb")
         nc.sync.dma_start(
             out=x_sb[:].rearrange("q b (u e) n -> q b u (e n)", u=HALVES),
             in_=x.rearrange("b (u q e) h w -> q b u (e h w)", u=HALVES, q=P),
         )
         for g in range(N_CHUNKS):
-            rows = memory[g * CHUNK : (g + 1) * CHUNK, :]
-            nc.sync.dma_start(out=mn[g][:], in_=rows.rearrange("(p t) c -> p t c", t=PACK))
+            rows = memory[g * CHUNK : (g + 1) * CHUNK, :].rearrange("(p t) c -> p t c", t=PACK)
+            if g == 0:
+                for t in range(PACK):
+                    nc.sync.dma_start(out=mn[g][:, t, :], in_=rows[:, t, :])
+            else:
+                nc.sync.dma_start(out=mn[g][:], in_=rows)
 
         make_identity(nc, ident[:])
         nc.vector.memset(ones[:], 1.0)
@@ -91,10 +101,12 @@ def tile_memorybank2d_pa_k_kernel(tc, x, memory, out_0, out_1):
         ):
             x_sq = prep.tile([P, BATCH, PACK, HW], F32, name="x_sq")
             x_part = prep.tile([P, BATCH, HW], F32, name="x_part")
-            x_norm = prep.tile([P, BATCH, HW], F32, name="x_norm")
-            x_inv = prep.tile([P, BATCH, HW], F32, name="x_inv")
+            x_norm = prep.tile([P, BATCH], F32, name="x_norm")
+            x_floored = prep.tile([P, BATCH], F32, name="x_floored")
+            x_inv = prep.tile([P, BATCH], F32, name="x_inv")
             fn_grouped = prep.tile([P, BATCH, HW, PACK], BF16, name="fn_grouped", align_bytes=64)
-            x_total = ps_words.tile([P, BATCH, HW], F32, name="x_total", tag="words")
+            x_total = ps_words.tile([P, BATCH, P], F32, name="x_total", tag="words")
+            x_inv_rows = ps_words.tile([P, BATCH, HW], F32, name="x_inv_rows", tag="words")
 
             def pixel_square_sums():
                 nc.vector.tensor_tensor(out=x_sq[:], in0=x_sb[:], in1=x_sb[:], op=ALU.mult)
@@ -104,21 +116,25 @@ def tile_memorybank2d_pa_k_kernel(tc, x, memory, out_0, out_1):
                     axis=AXIS.X,
                     op=ALU.add,
                 )
-                nc.tensor.matmul(
-                    out=x_total[:].rearrange("q b n -> q (b n)"),
-                    lhsT=ones[:],
-                    rhs=x_part[:].rearrange("q b n -> q (b n)"),
-                    start=True,
-                    stop=True,
-                )
+                for b in range(BATCH):
+                    nc.tensor.matmul(
+                        out=x_total[:, b, :], lhsT=x_part[:, b, :], rhs=ones[:], start=True, stop=True
+                    )
+
+            def pixel_norms():
+                nc.scalar.activation(out=x_norm[:], in_=x_total[:, :, 0], func=ACT.Sqrt)
+                nc.gpsimd.tensor_scalar_max(out=x_floored[:], in0=x_norm[:], scalar1=EPS)
+
+            def invert_pixel_norms():
+                nc.vector.reciprocal(out=x_inv[:], in_=x_floored[:])
+                for b in range(BATCH):
+                    spread_column(x_inv_rows[:, b, :], x_inv[:, b : b + 1])
 
             def pixel_codes():
-                nc.vector.tensor_scalar_max(out=x_norm[:], in0=x_norm[:], scalar1=EPS)
-                nc.vector.reciprocal(out=x_inv[:], in_=x_norm[:])
                 nc.vector.tensor_tensor(
                     out=fn_grouped[:],
                     in0=x_sb[:].rearrange("q b t n -> q b n t"),
-                    in1=x_inv[:].unsqueeze(3).to_broadcast([P, BATCH, HW, PACK]),
+                    in1=x_inv_rows[:].unsqueeze(3).to_broadcast([P, BATCH, HW, PACK]),
                     op=ALU.mult,
                 )
                 nc.vector.quantize_mx(
@@ -180,9 +196,16 @@ def tile_memorybank2d_pa_k_kernel(tc, x, memory, out_0, out_1):
                 nc.scalar.copy(
                     out=turned_words[g][:, 0], in_=word_banks[g][0][:].rearrange("q a e p -> q p e a")
                 )
-                nc.vector.tensor_copy(
-                    out=turned_words[g][:, 1], in_=word_banks[g][1][:].rearrange("q a e p -> q p e a")
-                )
+                if g % BOTH_TO_SCALAR_EVERY == 0:
+                    nc.scalar.copy(
+                        out=turned_words[g][:, 1],
+                        in_=word_banks[g][1][:].rearrange("q a e p -> q p e a"),
+                    )
+                else:
+                    nc.vector.tensor_copy(
+                        out=turned_words[g][:, 1],
+                        in_=word_banks[g][1][:].rearrange("q a e p -> q p e a"),
+                    )
 
             def quantise_turned(g):
                 nc.vector.quantize_mx(
@@ -213,20 +236,22 @@ def tile_memorybank2d_pa_k_kernel(tc, x, memory, out_0, out_1):
                 if is_chunk(r - 2):
                     scale_slots(r - 2)
                     turn_slots(r - 2)
+                if is_chunk(r - 1):
+                    invert_norms(r - 1)
+                if is_chunk(r - 4):
+                    quantise_turned(r - 4)
                 if is_chunk(r - 3):
                     collect_words(r - 3)
                 if is_chunk(r):
                     slot_norms(r)
-                if r == 0:
-                    nc.scalar.activation(out=x_norm[:], in_=x_total[:], func=ACT.Sqrt)
-                if is_chunk(r - 1):
-                    invert_norms(r - 1)
-                if r == 1:
-                    pixel_codes()
-                if is_chunk(r - 4):
-                    quantise_turned(r - 4)
                 if is_chunk(r - 5):
                     row_max(r - 5)
+                if r == 0:
+                    pixel_norms()
+                if r == 1:
+                    invert_pixel_norms()
+                if r == 2:
+                    pixel_codes()
 
             nc.scalar.activation(out=warm[:], in_=warm[:], func=ACT.Exp)
             nc.vector.tensor_reduce(out=neg_max[:], in_=chunk_max[:], axis=AXIS.X, op=ALU.max)
@@ -339,13 +364,7 @@ def tile_memorybank2d_pa_k_kernel(tc, x, memory, out_0, out_1):
             def spread_inverse_z():
                 rz_bank = ps_e.tile([P, BATCH, HW], F32, name="rz_bank", tag="sim")
                 for b in range(BATCH):
-                    nc.tensor.matmul(
-                        out=rz_bank[:, b, :],
-                        lhsT=rz[:, b : b + 1].to_broadcast([P, P]),
-                        rhs=ident[:],
-                        start=True,
-                        stop=True,
-                    )
+                    spread_column(rz_bank[:, b, :], rz[:, b : b + 1])
                 nc.scalar.copy(out=rz_rows[:], in_=rz_bank[:])
                 nc.sync.dma_start(
                     out=out_1.rearrange("(o b) h w -> o (b h w)", o=1),
@@ -366,8 +385,8 @@ def tile_memorybank2d_pa_k_kernel(tc, x, memory, out_0, out_1):
                 if is_chunk(r - 2):
                     group_slots(r - 2)
                 if is_chunk(r - 3):
-                    quantise_e(r - 3)
                     quantise_slots(r - 3)
+                    quantise_e(r - 3)
                 if r == N_CHUNKS:
                     invert_z()
                 if r == N_CHUNKS + 1:

@@ -23,7 +23,7 @@ N_CHUNKS = SLOTS // CHUNK
 C_TILES = CHANNELS // P
 PLANES_PER_TILE = 4
 EPS = 1e-12
-BOTH_TO_SCALAR_EVERY = 4
+ROWS_ON_GPSIMD = 2
 
 FLOPS = 2 * 2 * PIXELS * SLOTS * CHANNELS
 
@@ -171,8 +171,19 @@ def tile_memorybank2d_pa_k_kernel(tc, x, memory, out_0, out_1):
                 inverses[g] = stats.tile([P, PACK], F32, name="inverse")
                 nc.vector.reciprocal(out=inverses[g][:], in_=norms[g][:])
 
-            def scale_slots(g):
-                for t in range(PACK):
+            def scale_last_rows(g):
+                for t in range(PACK - ROWS_ON_GPSIMD, PACK):
+                    nc.gpsimd.tensor_scalar(
+                        out=mn[g][:, t, :],
+                        in0=mn[g][:, t, :],
+                        scalar1=inverses[g][:, t : t + 1],
+                        scalar2=0.0,
+                        op0=ALU.mult,
+                        op1=ALU.add,
+                    )
+
+            def scale_first_rows(g):
+                for t in range(PACK - ROWS_ON_GPSIMD):
                     nc.vector.tensor_scalar_mul(
                         out=mn[g][:, t, :], in0=mn[g][:, t, :], scalar1=inverses[g][:, t : t + 1]
                     )
@@ -196,16 +207,9 @@ def tile_memorybank2d_pa_k_kernel(tc, x, memory, out_0, out_1):
                 nc.scalar.copy(
                     out=turned_words[g][:, 0], in_=word_banks[g][0][:].rearrange("q a e p -> q p e a")
                 )
-                if g % BOTH_TO_SCALAR_EVERY == 0:
-                    nc.scalar.copy(
-                        out=turned_words[g][:, 1],
-                        in_=word_banks[g][1][:].rearrange("q a e p -> q p e a"),
-                    )
-                else:
-                    nc.vector.tensor_copy(
-                        out=turned_words[g][:, 1],
-                        in_=word_banks[g][1][:].rearrange("q a e p -> q p e a"),
-                    )
+                nc.vector.tensor_copy(
+                    out=turned_words[g][:, 1], in_=word_banks[g][1][:].rearrange("q a e p -> q p e a")
+                )
 
             def quantise_turned(g):
                 nc.vector.quantize_mx(
@@ -234,10 +238,11 @@ def tile_memorybank2d_pa_k_kernel(tc, x, memory, out_0, out_1):
                 if is_chunk(r):
                     slot_square_sums(r)
                 if is_chunk(r - 2):
-                    scale_slots(r - 2)
+                    scale_first_rows(r - 2)
                     turn_slots(r - 2)
                 if is_chunk(r - 1):
                     invert_norms(r - 1)
+                    scale_last_rows(r - 1)
                 if is_chunk(r - 4):
                     quantise_turned(r - 4)
                 if is_chunk(r - 3):

@@ -74,15 +74,16 @@ def tile_memorybank2d_pa_k_kernel(tc, x, memory, out_0, out_1):
             )
 
         x_sb = keep.tile([P, BATCH, PACK, HW], BF16, name="x_sb")
-        nc.sync.dma_start(
-            out=x_sb[:].rearrange("q b (u e) n -> q b u (e n)", u=HALVES),
-            in_=x.rearrange("b (u q e) h w -> q b u (e h w)", u=HALVES, q=P),
-        )
         for g in range(N_CHUNKS):
             rows = memory[g * CHUNK : (g + 1) * CHUNK, :].rearrange("(p t) c -> p t c", t=PACK)
             if g == 0:
                 for t in range(PACK):
                     nc.sync.dma_start(out=mn[g][:, t, :], in_=rows[:, t, :])
+                    if t == 0:
+                        nc.sync.dma_start(
+                            out=x_sb[:].rearrange("q b (u e) n -> q b u (e n)", u=HALVES),
+                            in_=x.rearrange("b (u q e) h w -> q b u (e h w)", u=HALVES, q=P),
+                        )
             else:
                 nc.sync.dma_start(out=mn[g][:], in_=rows)
 
@@ -200,14 +201,14 @@ def tile_memorybank2d_pa_k_kernel(tc, x, memory, out_0, out_1):
                             )
                     word_banks[g].append(bank)
 
-            def collect_words(g):
+            def collect_words(g, second_copy):
                 turned_words[g] = turned.tile(
                     [P, HALVES, P, 2, HALVES], F32, name="turned_words", align_bytes=64
                 )
                 nc.scalar.copy(
                     out=turned_words[g][:, 0], in_=word_banks[g][0][:].rearrange("q a e p -> q p e a")
                 )
-                nc.vector.tensor_copy(
+                second_copy(
                     out=turned_words[g][:, 1], in_=word_banks[g][1][:].rearrange("q a e p -> q p e a")
                 )
 
@@ -232,9 +233,9 @@ def tile_memorybank2d_pa_k_kernel(tc, x, memory, out_0, out_1):
                     )
 
             pixel_square_sums()
-            for r in range(N_CHUNKS + 5):
-                if is_chunk(r - 5):
-                    first_sim(r - 5)
+            for r in range(N_CHUNKS + 4):
+                if is_chunk(r - 4):
+                    first_sim(r - 4)
                 if is_chunk(r):
                     slot_square_sums(r)
                 if is_chunk(r - 2):
@@ -243,27 +244,30 @@ def tile_memorybank2d_pa_k_kernel(tc, x, memory, out_0, out_1):
                 if is_chunk(r - 1):
                     invert_norms(r - 1)
                     scale_last_rows(r - 1)
-                if is_chunk(r - 4):
-                    quantise_turned(r - 4)
                 if is_chunk(r - 3):
-                    collect_words(r - 3)
+                    quantise_turned(r - 3)
+                if is_chunk(r - 4):
+                    row_max(r - 4)
+                if is_chunk(r - 2):
+                    collect_words(r - 2, nc.vector.tensor_copy if is_chunk(r) else nc.scalar.copy)
                 if is_chunk(r):
                     slot_norms(r)
-                if is_chunk(r - 5):
-                    row_max(r - 5)
-                if r == 0:
-                    pixel_norms()
                 if r == 1:
-                    invert_pixel_norms()
+                    pixel_norms()
                 if r == 2:
+                    invert_pixel_norms()
+                if r == 3:
                     pixel_codes()
+                if r == N_CHUNKS:
+                    nc.scalar.activation(out=warm[:], in_=warm[:], func=ACT.Exp)
 
-            nc.scalar.activation(out=warm[:], in_=warm[:], func=ACT.Exp)
-            nc.vector.tensor_reduce(out=neg_max[:], in_=chunk_max[:], axis=AXIS.X, op=ALU.max)
-            nc.vector.tensor_scalar_mul(out=neg_max[:], in0=neg_max[:], scalar1=-1.0)
+            nc.vector.tensor_reduce(
+                out=neg_max[:], in_=chunk_max[:], axis=AXIS.X, op=ALU.max, negate=True
+            )
 
         with (
             tc.tile_pool(name="pairs", bufs=2, reuse_waits="tile") as pairs,
+            tc.tile_pool(name="ahead", bufs=3, reuse_waits="tile") as ahead,
             tc.tile_pool(name="last", bufs=1, reuse_waits="tile") as last,
             tc.psum_pool(name="ps_recon", bufs=1, reuse_waits="tile") as ps_recon,
             tc.psum_pool(name="ps_e", bufs=2, reuse_waits="tile") as ps_e,
@@ -327,7 +331,7 @@ def tile_memorybank2d_pa_k_kernel(tc, x, memory, out_0, out_1):
                 )
 
             def group_slots(g):
-                mn_grouped[g] = pairs.tile(
+                mn_grouped[g] = ahead.tile(
                     [P, CHANNELS, PACK], BF16, name="mn_grouped", align_bytes=64
                 )
                 nc.vector.tensor_copy(
@@ -376,22 +380,24 @@ def tile_memorybank2d_pa_k_kernel(tc, x, memory, out_0, out_1):
                     in_=rz_rows[0:1].rearrange("o b n -> o (b n)"),
                 )
 
-            for r in range(N_CHUNKS + 4):
-                if is_chunk(r):
-                    second_sim(r)
-                if is_chunk(r - 4):
-                    add_to_recon(r - 4)
+            second_sim(0)
+            group_slots(0)
+            for r in range(N_CHUNKS + 3):
                 if is_chunk(r - 1):
                     turn_e(r - 1)
-                if is_chunk(r - 2):
-                    collect_e(r - 2)
+                if is_chunk(r - 3):
+                    add_to_recon(r - 3)
                 if is_chunk(r):
                     exponentials(r)
+                if is_chunk(r + 1):
+                    second_sim(r + 1)
+                if is_chunk(r - 1):
+                    collect_e(r - 1)
                 if is_chunk(r - 2):
-                    group_slots(r - 2)
-                if is_chunk(r - 3):
-                    quantise_slots(r - 3)
-                    quantise_e(r - 3)
+                    quantise_slots(r - 2)
+                    quantise_e(r - 2)
+                if is_chunk(r + 1):
+                    group_slots(r + 1)
                 if r == N_CHUNKS:
                     invert_z()
                 if r == N_CHUNKS + 1:

@@ -24,13 +24,18 @@ C_TILES = CHANNELS // P
 PLANES_PER_TILE = 4
 EPS = 1e-12
 ROWS_ON_GPSIMD = 2
+CHANNELS_ON_SCALAR = 32
 
 FLOPS = 2 * 2 * PIXELS * SLOTS * CHANNELS
 
 
 def tile_memorybank2d_pa_k_kernel(tc, x, memory, out_0, out_1):
     nc = tc.nc
-    with tc.manual_schedule(), tc.tile_pool(name="keep", bufs=1) as keep:
+    with (
+        tc.manual_schedule(),
+        tc.tile_pool(name="keep", bufs=1) as keep,
+        tc.tile_pool(name="ahead", bufs=3) as ahead,
+    ):
         ident = keep.tile([P, P], F32, name="ident")
         ones = keep.tile([P, P], F32, name="ones")
         warm = keep.tile([P, 1], F32, name="warm")
@@ -72,6 +77,20 @@ def tile_memorybank2d_pa_k_kernel(tc, x, memory, out_0, out_1):
             nc.tensor.matmul(
                 out=rows, lhsT=column.to_broadcast([P, P]), rhs=ident[:], start=True, stop=True
             )
+
+        mn_grouped = {}
+
+        def group_share(copy, g, first, last):
+            copy(
+                out=mn_grouped[g][:, first:last, :].rearrange("p (c i) t -> p c t i", i=4),
+                in_=mn[g][:, :, first:last].rearrange("p t (c i) -> p c t i", i=4),
+            )
+
+        def group_slots(g, on_scalar):
+            mn_grouped[g] = ahead.tile([P, CHANNELS, PACK], BF16, name="mn_grouped", align_bytes=64)
+            group_share(nc.scalar.copy, g, 0, on_scalar)
+            if on_scalar < CHANNELS:
+                group_share(nc.vector.tensor_copy, g, on_scalar, CHANNELS)
 
         x_sb = keep.tile([P, BATCH, PACK, HW], BF16, name="x_sb")
         for g in range(N_CHUNKS):
@@ -261,13 +280,13 @@ def tile_memorybank2d_pa_k_kernel(tc, x, memory, out_0, out_1):
                 if r == N_CHUNKS:
                     nc.scalar.activation(out=warm[:], in_=warm[:], func=ACT.Exp)
 
+            group_slots(0, CHANNELS)
             nc.vector.tensor_reduce(
                 out=neg_max[:], in_=chunk_max[:], axis=AXIS.X, op=ALU.max, negate=True
             )
 
         with (
             tc.tile_pool(name="pairs", bufs=2, reuse_waits="tile") as pairs,
-            tc.tile_pool(name="ahead", bufs=3, reuse_waits="tile") as ahead,
             tc.tile_pool(name="last", bufs=1, reuse_waits="tile") as last,
             tc.psum_pool(name="ps_recon", bufs=1, reuse_waits="tile") as ps_recon,
             tc.psum_pool(name="ps_e", bufs=2, reuse_waits="tile") as ps_e,
@@ -281,7 +300,6 @@ def tile_memorybank2d_pa_k_kernel(tc, x, memory, out_0, out_1):
             eT_words = {}
             eT_codes = {}
             eT_scales = {}
-            mn_grouped = {}
             mn_codes = {}
             mn_scales = {}
 
@@ -330,15 +348,6 @@ def tile_memorybank2d_pa_k_kernel(tc, x, memory, out_0, out_1):
                     in_=eT_words[g][:].rearrange("j b n a -> j (b n a)").bitcast(BF16),
                 )
 
-            def group_slots(g):
-                mn_grouped[g] = ahead.tile(
-                    [P, CHANNELS, PACK], BF16, name="mn_grouped", align_bytes=64
-                )
-                nc.vector.tensor_copy(
-                    out=mn_grouped[g][:].rearrange("p (c i) t -> p c t i", i=4),
-                    in_=mn[g][:].rearrange("p t (c i) -> p c t i", i=4),
-                )
-
             def quantise_slots(g):
                 mn_codes[g] = pairs.tile([P, CHANNELS], U32, name="mn_codes", align_bytes=64)
                 mn_scales[g] = pairs.tile([P, CHANNELS], U8, name="mn_scales", align_bytes=64)
@@ -381,7 +390,6 @@ def tile_memorybank2d_pa_k_kernel(tc, x, memory, out_0, out_1):
                 )
 
             second_sim(0)
-            group_slots(0)
             for r in range(N_CHUNKS + 3):
                 if is_chunk(r - 1):
                     turn_e(r - 1)
@@ -397,7 +405,7 @@ def tile_memorybank2d_pa_k_kernel(tc, x, memory, out_0, out_1):
                     quantise_slots(r - 2)
                     quantise_e(r - 2)
                 if is_chunk(r + 1):
-                    group_slots(r + 1)
+                    group_slots(r + 1, CHANNELS_ON_SCALAR)
                 if r == N_CHUNKS:
                     invert_z()
                 if r == N_CHUNKS + 1:

import concourse.mybir as mybir
from concourse.masks import make_identity

F32 = mybir.dt.float32
BF16 = mybir.dt.bfloat16
U32 = mybir.dt.uint32
U8 = mybir.dt.uint8
FP8X4 = mybir.dt.float8_e4m3fn_x4
ACT = mybir.ActivationFunctionType
ALU = mybir.AluOpType
AXIS = mybir.AxisListType

P = 128
PACK = 4
HALVES = 2
BATCH = 2
CHANNELS = 512
HW = 128
PIXELS = BATCH * HW
SLOTS = 16384
CHUNK = P * PACK
N_CHUNKS = SLOTS // CHUNK
C_TILES = CHANNELS // P
PLANES_PER_TILE = 4
EPS = 1e-12
ROWS_ON_GPSIMD = 2
CHANNELS_ON_SCALAR = 32

FLOPS = 2 * 2 * PIXELS * SLOTS * CHANNELS


def tile_memorybank2d_pa_k_kernel(tc, x, memory, out_0, out_1):
    nc = tc.nc
    with (
        tc.manual_schedule(),
        tc.tile_pool(name="keep", bufs=1) as keep,
        tc.tile_pool(name="ahead", bufs=3) as ahead,
    ):
        ident = keep.tile([P, P], F32, name="ident")
        ones = keep.tile([P, P], F32, name="ones")
        warm = keep.tile([P, 1], F32, name="warm")
        fn_codes = keep.tile([P, PIXELS], U32, name="fn_codes", align_bytes=64)
        fn_scales = keep.tile([P, PIXELS], U8, name="fn_scales", align_bytes=64)
        chunk_max = keep.tile([P, BATCH, N_CHUNKS], F32, name="chunk_max")
        chunk_z = keep.tile([P, BATCH, N_CHUNKS], F32, name="chunk_z")
        neg_max = keep.tile([P, BATCH], F32, name="neg_max")
        mn = [keep.tile([P, PACK, CHANNELS], BF16, name="mn%d" % g) for g in range(N_CHUNKS)]
        mnT_codes = [
            keep.tile([P, CHUNK], U32, name="mnT_codes%d" % g, align_bytes=64)
            for g in range(N_CHUNKS)
        ]
        mnT_planes = [
            keep.tile([P, CHUNK], U8, name="mnT_planes%d" % j, align_bytes=64)
            for j in range(N_CHUNKS // PLANES_PER_TILE)
        ]

        def is_chunk(g):
            return 0 <= g < N_CHUNKS

        def mnT_scales(g):
            first_row = PACK * (g % PLANES_PER_TILE)
            return mnT_planes[g // PLANES_PER_TILE][first_row:P, :]

        def sim_pass(bank, g, b):
            pixels = slice(b * HW, (b + 1) * HW)
            nc.tensor.matmul_mx(
                out=bank,
                lhsT=fn_codes[:, pixels].bitcast(FP8X4),
                lhsT_scale=fn_scales[:, pixels],
                rhs=mnT_codes[g][:].bitcast(FP8X4),
                rhs_scale=mnT_scales(g),
                start=True,
                stop=True,
            )

        def spread_column(rows, column):
            nc.tensor.matmul(
                out=rows, lhsT=column.to_broadcast([P, P]), rhs=ident[:], start=True, stop=True
            )

        mn_grouped = {}

        def group_share(copy, g, first, last):
            copy(
                out=mn_grouped[g][:, first:last, :].rearrange("p (c i) t -> p c t i", i=4),
                in_=mn[g][:, :, first:last].rearrange("p t (c i) -> p c t i", i=4),
            )

        def group_slots(g, on_scalar):
            mn_grouped[g] = ahead.tile([P, CHANNELS, PACK], BF16, name="mn_grouped", align_bytes=64)
            group_share(nc.scalar.copy, g, 0, on_scalar)
            if on_scalar < CHANNELS:
                group_share(nc.vector.tensor_copy, g, on_scalar, CHANNELS)

        x_sb = keep.tile([P, BATCH, PACK, HW], BF16, name="x_sb")
        for g in range(N_CHUNKS):
            rows = memory[g * CHUNK : (g + 1) * CHUNK, :].rearrange("(p t) c -> p t c", t=PACK)
            if g == 0:
                for t in range(PACK):
                    nc.sync.dma_start(out=mn[g][:, t, :], in_=rows[:, t, :])
                    if t == 0:
                        nc.sync.dma_start(
                            out=x_sb[:].rearrange("q b (u e) n -> q b u (e n)", u=HALVES),
                            in_=x.rearrange("b (u q e) h w -> q b u (e h w)", u=HALVES, q=P),
                        )
            else:
                nc.sync.dma_start(out=mn[g][:], in_=rows)

        make_identity(nc, ident[:])
        nc.vector.memset(ones[:], 1.0)
        nc.vector.memset(warm[:], 1.0)
        nc.scalar.activation(out=warm[:], in_=warm[:], func=ACT.Sqrt)

        with (
            tc.tile_pool(name="prep", bufs=1) as prep,
            tc.tile_pool(name="stats", bufs=4) as stats,
            tc.tile_pool(name="squares", bufs=4) as squares,
            tc.tile_pool(name="turned", bufs=3) as turned,
            tc.psum_pool(name="ps_words", bufs=4) as ps_words,
            tc.psum_pool(name="ps_sim", bufs=4) as ps_sim,
        ):
            x_sq = prep.tile([P, BATCH, PACK, HW], F32, name="x_sq")
            x_part = prep.tile([P, BATCH, HW], F32, name="x_part")
            x_norm = prep.tile([P, BATCH], F32, name="x_norm")
            x_floored = prep.tile([P, BATCH], F32, name="x_floored")
            x_inv = prep.tile([P, BATCH], F32, name="x_inv")
            fn_grouped = prep.tile([P, BATCH, HW, PACK], BF16, name="fn_grouped", align_bytes=64)
            x_total = ps_words.tile([P, BATCH, P], F32, name="x_total", tag="words")
            x_inv_rows = ps_words.tile([P, BATCH, HW], F32, name="x_inv_rows", tag="words")

            def pixel_square_sums():
                nc.vector.tensor_tensor(out=x_sq[:], in0=x_sb[:], in1=x_sb[:], op=ALU.mult)
                nc.vector.tensor_reduce(
                    out=x_part[:],
                    in_=x_sq[:].rearrange("q b t n -> q b n t"),
                    axis=AXIS.X,
                    op=ALU.add,
                )
                for b in range(BATCH):
                    nc.tensor.matmul(
                        out=x_total[:, b, :], lhsT=x_part[:, b, :], rhs=ones[:], start=True, stop=True
                    )

            def pixel_norms():
                nc.scalar.activation(out=x_norm[:], in_=x_total[:, :, 0], func=ACT.Sqrt)
                nc.gpsimd.tensor_scalar_max(out=x_floored[:], in0=x_norm[:], scalar1=EPS)

            def invert_pixel_norms():
                nc.vector.reciprocal(out=x_inv[:], in_=x_floored[:])
                for b in range(BATCH):
                    spread_column(x_inv_rows[:, b, :], x_inv[:, b : b + 1])

            def pixel_codes():
                nc.vector.tensor_tensor(
                    out=fn_grouped[:],
                    in0=x_sb[:].rearrange("q b t n -> q b n t"),
                    in1=x_inv_rows[:].unsqueeze(3).to_broadcast([P, BATCH, HW, PACK]),
                    op=ALU.mult,
                )
                nc.vector.quantize_mx(
                    out=fn_codes[:].bitcast(FP8X4),
                    scales=fn_scales[:],
                    in_=fn_grouped[:].rearrange("q b n t -> q (b n t)"),
                )

            square_sums = {}
            norms = {}
            inverses = {}
            word_banks = {}
            turned_words = {}
            sim_banks = {}

            def slot_square_sums(g):
                square_sums[g] = stats.tile([P, PACK], F32, name="square_sum")
                for t in range(PACK):
                    unread = squares.tile([P, CHANNELS], BF16, name="unread")
                    nc.scalar.activation(
                        out=unread[:],
                        in_=mn[g][:, t, :],
                        func=ACT.Square,
                        accum_out=square_sums[g][:, t : t + 1],
                    )

            def slot_norms(g):
                norm = stats.tile([P, PACK], F32, name="norm")
                norms[g] = stats.tile([P, PACK], F32, name="floored")
                nc.scalar.activation(out=norm[:], in_=square_sums[g][:], func=ACT.Sqrt)
                nc.gpsimd.tensor_scalar_max(out=norms[g][:], in0=norm[:], scalar1=EPS)

            def invert_norms(g):
                inverses[g] = stats.tile([P, PACK], F32, name="inverse")
                nc.vector.reciprocal(out=inverses[g][:], in_=norms[g][:])

            def scale_last_rows(g):
                for t in range(PACK - ROWS_ON_GPSIMD, PACK):
                    nc.gpsimd.tensor_scalar(
                        out=mn[g][:, t, :],
                        in0=mn[g][:, t, :],
                        scalar1=inverses[g][:, t : t + 1],
                        scalar2=0.0,
                        op0=ALU.mult,
                        op1=ALU.add,
                    )

            def scale_first_rows(g):
                for t in range(PACK - ROWS_ON_GPSIMD):
                    nc.vector.tensor_scalar_mul(
                        out=mn[g][:, t, :], in0=mn[g][:, t, :], scalar1=inverses[g][:, t : t + 1]
                    )

            def turn_slots(g):
                words = mn[g][:].bitcast(F32)
                word_banks[g] = []
                for u in range(HALVES):
                    bank = ps_words.tile([P, HALVES, 2, P], F32, name="words")
                    for a in range(HALVES):
                        for e in range(2):
                            nc.tensor.transpose(
                                bank[:, a, e, :], words[:, 2 * u + e, a * P : (a + 1) * P], ident[:]
                            )
                    word_banks[g].append(bank)

            def collect_words(g, second_copy):
                turned_words[g] = turned.tile(
                    [P, HALVES, P, 2, HALVES], F32, name="turned_words", align_bytes=64
                )
                nc.scalar.copy(
                    out=turned_words[g][:, 0], in_=word_banks[g][0][:].rearrange("q a e p -> q p e a")
                )
                second_copy(
                    out=turned_words[g][:, 1], in_=word_banks[g][1][:].rearrange("q a e p -> q p e a")
                )

            def quantise_turned(g):
                nc.vector.quantize_mx(
                    out=mnT_codes[g][:].bitcast(FP8X4),
                    scales=mnT_scales(g),
                    in_=turned_words[g][:].rearrange("q u p e a -> q (u p e a)").bitcast(BF16),
                )

            def first_sim(g):
                sim_banks[g] = []
                for b in range(BATCH):
                    bank = ps_sim.tile([P, CHUNK], F32, name="sim")
                    sim_pass(bank[:], g, b)
                    sim_banks[g].append(bank)

            def row_max(g):
                for b in range(BATCH):
                    nc.vector.tensor_reduce(
                        out=chunk_max[:, b, g : g + 1], in_=sim_banks[g][b][:], axis=AXIS.X, op=ALU.max
                    )

            pixel_square_sums()
            for r in range(N_CHUNKS + 4):
                if is_chunk(r - 4):
                    first_sim(r - 4)
                if is_chunk(r):
                    slot_square_sums(r)
                if is_chunk(r - 2):
                    scale_first_rows(r - 2)
                    turn_slots(r - 2)
                if is_chunk(r - 1):
                    invert_norms(r - 1)
                    scale_last_rows(r - 1)
                if is_chunk(r - 3):
                    quantise_turned(r - 3)
                if is_chunk(r - 4):
                    row_max(r - 4)
                if is_chunk(r - 2):
                    collect_words(r - 2, nc.vector.tensor_copy if is_chunk(r) else nc.scalar.copy)
                if is_chunk(r):
                    slot_norms(r)
                if r == 1:
                    pixel_norms()
                if r == 2:
                    invert_pixel_norms()
                if r == 3:
                    pixel_codes()
                if r == N_CHUNKS:
                    nc.scalar.activation(out=warm[:], in_=warm[:], func=ACT.Exp)

            group_slots(0, CHANNELS)
            nc.vector.tensor_reduce(
                out=neg_max[:], in_=chunk_max[:], axis=AXIS.X, op=ALU.max, negate=True
            )

        with (
            tc.tile_pool(name="pairs", bufs=2, reuse_waits="tile") as pairs,
            tc.tile_pool(name="last", bufs=1, reuse_waits="tile") as last,
            tc.psum_pool(name="ps_recon", bufs=1, reuse_waits="tile") as ps_recon,
            tc.psum_pool(name="ps_e", bufs=2, reuse_waits="tile") as ps_e,
        ):
            recon_banks = [
                ps_recon.tile([P, BATCH, HW], F32, name="recon%d" % k) for k in range(C_TILES)
            ]
            sim_banks = {}
            e_tiles = {}
            eT_banks = {}
            eT_words = {}
            eT_codes = {}
            eT_scales = {}
            mn_codes = {}
            mn_scales = {}

            def second_sim(g):
                sim_banks[g] = []
                for b in range(BATCH):
                    bank = ps_e.tile([P, CHUNK], F32, name="sim")
                    sim_pass(bank[:], g, b)
                    sim_banks[g].append(bank)

            def exponentials(g):
                e_tiles[g] = []
                for b in range(BATCH):
                    e_tile = pairs.tile([P, CHUNK], BF16, name="e%d" % b)
                    nc.scalar.activation(
                        out=e_tile[:],
                        in_=sim_banks[g][b][:],
                        func=ACT.Exp,
                        bias=neg_max[:, b : b + 1],
                        scale=1.0,
                        accum_out=chunk_z[:, b, g : g + 1],
                    )
                    e_tiles[g].append(e_tile)

            def turn_e(g):
                eT_banks[g] = ps_e.tile([P, HALVES, BATCH, HW], F32, name="eT")
                for b in range(BATCH):
                    words = e_tiles[g][b][:].bitcast(F32)
                    for a in range(HALVES):
                        nc.tensor.transpose(
                            eT_banks[g][:, a, b, :], words[:, a * P : (a + 1) * P], ident[:]
                        )

            def collect_e(g):
                eT_words[g] = pairs.tile(
                    [P, BATCH, HW, HALVES], F32, name="eT_words", align_bytes=64
                )
                nc.scalar.copy(out=eT_words[g][:], in_=eT_banks[g][:].rearrange("j a b n -> j b n a"))

            def quantise_e(g):
                eT_codes[g] = pairs.tile([P, PIXELS], U32, name="eT_codes", align_bytes=64)
                eT_scales[g] = pairs.tile([P, PIXELS], U8, name="eT_scales", align_bytes=64)
                nc.vector.quantize_mx(
                    out=eT_codes[g][:].bitcast(FP8X4),
                    scales=eT_scales[g][:],
                    in_=eT_words[g][:].rearrange("j b n a -> j (b n a)").bitcast(BF16),
                )

            def quantise_slots(g):
                mn_codes[g] = pairs.tile([P, CHANNELS], U32, name="mn_codes", align_bytes=64)
                mn_scales[g] = pairs.tile([P, CHANNELS], U8, name="mn_scales", align_bytes=64)
                nc.vector.quantize_mx(
                    out=mn_codes[g][:].bitcast(FP8X4),
                    scales=mn_scales[g][:],
                    in_=mn_grouped[g][:].rearrange("p c t -> p (c t)"),
                )

            def add_to_recon(g):
                for k in range(C_TILES):
                    channels = slice(k * P, (k + 1) * P)
                    nc.tensor.matmul_mx(
                        out=recon_banks[k][:].rearrange("c b n -> c (b n)"),
                        lhsT=mn_codes[g][:, channels].bitcast(FP8X4),
                        lhsT_scale=mn_scales[g][:, channels],
                        rhs=eT_codes[g][:].bitcast(FP8X4),
                        rhs_scale=eT_scales[g][:],
                        start=(g == 0),
                        stop=(g == N_CHUNKS - 1),
                    )

            rz_rows = last.tile([P, BATCH, HW], F32, name="rz_rows")

            z = last.tile([P, BATCH], F32, name="z")
            rz = last.tile([P, BATCH], F32, name="rz")

            def invert_z():
                nc.vector.tensor_reduce(out=z[:], in_=chunk_z[:], axis=AXIS.X, op=ALU.add)
                nc.vector.reciprocal(out=rz[:], in_=z[:])

            def spread_inverse_z():
                rz_bank = ps_e.tile([P, BATCH, HW], F32, name="rz_bank", tag="sim")
                for b in range(BATCH):
                    spread_column(rz_bank[:, b, :], rz[:, b : b + 1])
                nc.scalar.copy(out=rz_rows[:], in_=rz_bank[:])
                nc.sync.dma_start(
                    out=out_1.rearrange("(o b) h w -> o (b h w)", o=1),
                    in_=rz_rows[0:1].rearrange("o b n -> o (b n)"),
                )

            second_sim(0)
            for r in range(N_CHUNKS + 3):
                if is_chunk(r - 1):
                    turn_e(r - 1)
                if is_chunk(r - 3):
                    add_to_recon(r - 3)
                if is_chunk(r):
                    exponentials(r)
                if is_chunk(r + 1):
                    second_sim(r + 1)
                if is_chunk(r - 1):
                    collect_e(r - 1)
                if is_chunk(r - 2):
                    quantise_slots(r - 2)
                    quantise_e(r - 2)
                if is_chunk(r + 1):
                    group_slots(r + 1, CHANNELS_ON_SCALAR)
                if r == N_CHUNKS:
                    invert_z()
                if r == N_CHUNKS + 1:
                    spread_inverse_z()

            out_tiles = out_0.rearrange("b (k c) h w -> k c b (h w)", c=P)
            for k in range(C_TILES):
                recon = last.tile([P, BATCH, HW], F32, name="recon_out%d" % k)
                nc.vector.tensor_tensor(
                    out=recon[:], in0=recon_banks[k][:], in1=rz_rows[:], op=ALU.mult
                )
                nc.sync.dma_start(out=out_tiles[k], in_=recon[:])
